import numpy as np
import ml_dtypes

BF16 = ml_dtypes.bfloat16


def bf(x):
    return np.asarray(x, np.float32).astype(BF16)


def f32(x):
    return np.asarray(x, np.float32)


def f64(x):
    return np.asarray(x).astype(np.float64)


def striped(idx):
    return np.tile(idx.reshape(-1, 16).T, (8, 1))


B, E, P, D, S, N = 16, 512, 128, 128, 4096, 2048
SCALE = 0.08838834764831845
VSCALE = 4.0


def attn_lse(qb, kb, vb, mask):
    sc = (qb.transpose(0, 2, 1) @ kb) * SCALE
    if mask is not None:
        sc = np.where(mask, sc, -np.inf)
    m = sc.max(axis=-1, keepdims=True)
    p = np.exp(sc - m)
    den = p.sum(axis=-1, keepdims=True)
    o = vb.transpose(0, 2, 1) @ (p / den).transpose(0, 2, 1)
    return o, (m + np.log(den))[:, :, 0]


def setup_inputs():
    return {
        "table": bf(np.random.standard_normal((D, S))),
        "q": bf(np.random.standard_normal((B, D, E))),
        "k": bf(np.random.standard_normal((B, D, E))),
        "v": bf(VSCALE * np.random.standard_normal((B, E, D))),
        "vp": bf(VSCALE * np.random.standard_normal((B, P, D))),
        "offs": striped(np.random.permutation(S)[:N]),
    }


def reference(table, q, k, v, vp, offs):
    idx = offs[:16].T.reshape(-1)
    kp = f64(table)[:, idx].reshape(D, B, P).transpose(1, 0, 2)
    causal = np.tril(np.ones((E, E), bool))
    o1, s1 = attn_lse(f64(q), f64(k), f64(v), causal)
    o2, s2 = attn_lse(f64(q), kp, f64(vp), None)
    mx = np.maximum(s1, s2)
    s = mx + np.log(np.exp(s1 - mx) + np.exp(s2 - mx))
    return o1 * np.exp(s1 - s)[:, None, :] + o2 * np.exp(s2 - s)[:, None, :]

@@ -1,0 +1,152 @@
+import concourse.mybir as mybir
+from concourse.masks import make_identity
+
+F32 = mybir.dt.float32
+BF16 = mybir.dt.bfloat16
+U16 = mybir.dt.uint16
+ALU = mybir.AluOpType
+EXP = mybir.ActivationFunctionType.Exp
+
+REQUESTS = 16
+TOKENS = 512
+PREFIX = 128
+FEATURES = 128
+SLOTS = 4096
+BLOCK = 128
+QBLOCKS = TOKENS // BLOCK
+GROUP = 4
+SCALE = 0.08838834764831845
+MASKED = -1.0e30
+LAG = 2
+
+FLOPS = REQUESTS * 2 * 2 * FEATURES * (TOKENS * (TOKENS + 1) // 2 + TOKENS * PREFIX)
+
+
+def tile_radixattention_b_kernel(tc, table, q, k, v, vp, offs, out):
+    nc = tc.nc
+    with (
+        tc.tile_pool(name="held", bufs=1) as held,
+        tc.tile_pool(name="rows", bufs=2 * GROUP) as rows,
+        tc.tile_pool(name="work", bufs=3) as work,
+        tc.psum_pool(name="arena", bufs=1) as arena_pool,
+        tc.psum_pool(name="flipped", bufs=4) as flipped_pool,
+    ):
+        offsets = held.tile([128, REQUESTS * PREFIX // 16], U16, name="offsets")
+        nc.sync.dma_start(offsets[:], offs)
+        pool_sb = held.tile([FEATURES, SLOTS], BF16, name="pool_sb")
+
+        q_sb, k_sb, v_sb, vp_sb = [], [], [], []
+        for g in range(REQUESTS // GROUP):
+            first, last = g * GROUP, (g + 1) * GROUP
+            q_sb.append(held.tile([FEATURES, GROUP, TOKENS], BF16, name=f"q{g}"))
+            k_sb.append(held.tile([FEATURES, GROUP, TOKENS], BF16, name=f"k{g}"))
+            v_sb.append(held.tile([BLOCK, GROUP * QBLOCKS, FEATURES], BF16, name=f"v{g}"))
+            vp_sb.append(held.tile([PREFIX, GROUP, FEATURES], BF16, name=f"vp{g}"))
+            nc.sync.dma_start(q_sb[g][:], q[first:last].rearrange("b d e -> d b e"))
+            if g == 0:
+                nc.sync.dma_start(pool_sb[:], table)
+            nc.sync.dma_start(k_sb[g][:], k[first:last].rearrange("b d t -> d b t"))
+            nc.sync.dma_start(v_sb[g][:], v[first:last].rearrange("b (j p) d -> p (b j) d", p=BLOCK))
+            nc.sync.dma_start(vp_sb[g][:], vp[first:last].rearrange("b r d -> r b d"))
+
+        identity = held.tile([BLOCK, BLOCK], BF16, name="identity")
+        make_identity(nc, identity[:])
+        causal = held.tile([BLOCK, BLOCK], BF16, name="causal")
+        nc.gpsimd.memset(causal[:], 0.0)
+        nc.gpsimd.affine_select(
+            out=causal[:], in_=causal[:], compare_op=ALU.is_ge, fill=MASKED,
+            base=0, pattern=[[-1, BLOCK]], channel_multiplier=1,
+        )
+
+        negated, prefix_low, weights = {}, {}, {}
+
+        def query_block(b, i):
+            return q_sb[b // GROUP][:, b % GROUP, i * BLOCK : (i + 1) * BLOCK]
+
+        def prefix_scores(g):
+            prefix_ps = arena_pool.tile([BLOCK, GROUP, TOKENS], F32, tag="arena", name="prefix_ps")
+            for r in range(GROUP):
+                b = g * GROUP + r
+                page_table = offsets[:, b * PREFIX // 16 : (b + 1) * PREFIX // 16]
+                for i in range(QBLOCKS):
+                    nc.tensor.matmul(
+                        prefix_ps[:, r, i * BLOCK : (i + 1) * BLOCK],
+                        query_block(b, i),
+                        pool_sb[:].indirect(page_table),
+                        start=True, stop=True,
+                    )
+            for r in range(GROUP):
+                b = g * GROUP + r
+                negated[b] = [
+                    rows.tile([BLOCK, PREFIX + (i + 1) * BLOCK], F32, name=f"negated{i}")
+                    for i in range(QBLOCKS)
+                ]
+                prefix_low[b] = rows.tile([BLOCK, QBLOCKS], F32, name="prefix_low")
+                for i in range(QBLOCKS):
+                    nc.vector.tensor_scalar(
+                        out=negated[b][i][:, 0:PREFIX],
+                        in0=prefix_ps[:, r, i * BLOCK : (i + 1) * BLOCK],
+                        scalar1=-SCALE, scalar2=None, op0=ALU.mult, op1=ALU.min,
+                        accum_out=prefix_low[b][:, i : i + 1],
+                    )
+
+        def softmax_rows(b, arena):
+            keys = k_sb[b // GROUP][:, b % GROUP, :]
+            low = rows.tile([BLOCK, QBLOCKS], F32, name="low")
+            total = rows.tile([BLOCK, QBLOCKS], F32, name="total")
+            exps = []
+            for i in range(QBLOCKS):
+                width = (i + 1) * BLOCK
+                bank = (b * QBLOCKS + i) % 3
+                nc.tensor.matmul(arena[:, bank, 0:width], query_block(b, i), keys[:, 0:width], start=True, stop=False)
+                nc.tensor.matmul(arena[:, bank, i * BLOCK : width], identity[:], causal[:], start=False, stop=True)
+                nc.vector.tensor_scalar(
+                    out=negated[b][i][:, PREFIX : PREFIX + width],
+                    in0=arena[:, bank, 0:width],
+                    scalar1=-SCALE, scalar2=prefix_low[b][:, i : i + 1], op0=ALU.mult, op1=ALU.min,
+                    accum_out=low[:, i : i + 1],
+                )
+                exps.append(work.tile([BLOCK, PREFIX + width], F32, name=f"exps{i}"))
+                nc.scalar.activation(
+                    out=exps[i][:], in_=negated[b][i][:], func=EXP,
+                    bias=low[:, i : i + 1], scale=-1.0, accum_out=total[:, i : i + 1],
+                )
+            factor = rows.tile([BLOCK, QBLOCKS], F32, name="factor")
+            nc.vector.reciprocal(factor[:], total[:])
+            weights[b] = []
+            for i in range(QBLOCKS):
+                weights[b].append(work.tile([BLOCK, PREFIX + (i + 1) * BLOCK], BF16, name=f"weights{i}"))
+                nc.gpsimd.tensor_scalar(
+                    out=weights[b][i][:], in0=exps[i][:],
+                    scalar1=factor[:, i : i + 1], scalar2=1.0, op0=ALU.mult, op1=ALU.mult,
+                )
+
+        def weighted_values(b, arena):
+            flipped = work.tile([BLOCK, 1 + QBLOCKS, TOKENS], BF16, name="flipped")
+            for i in range(QBLOCKS):
+                flipped_ps = flipped_pool.tile([BLOCK, 1 + QBLOCKS, BLOCK], BF16, name="flipped_ps")
+                for j in range(i + 2):
+                    nc.tensor.transpose(flipped_ps[:, j, :], weights[b][i][:, j * BLOCK : (j + 1) * BLOCK], identity[:])
+                nc.scalar.copy(out=flipped[:, 0 : i + 2, i * BLOCK : (i + 1) * BLOCK], in_=flipped_ps[:, 0 : i + 2, :])
+            out_ps = arena[:, 3, :]
+            nc.tensor.matmul(out_ps, vp_sb[b // GROUP][:, b % GROUP, :], flipped[:, 0, :], start=True, stop=False)
+            for j in range(QBLOCKS):
+                nc.tensor.matmul(
+                    arena[:, 3, j * BLOCK : TOKENS],
+                    v_sb[b // GROUP][:, (b % GROUP) * QBLOCKS + j, :],
+                    flipped[:, 1 + j, j * BLOCK : TOKENS],
+                    start=False, stop=(j == QBLOCKS - 1),
+                )
+            out_sb = work.tile([FEATURES, TOKENS], F32, name="out_sb")
+            nc.vector.tensor_copy(out_sb[:], out_ps)
+            nc.sync.dma_start(out[b], out_sb[:])
+
+        arena = None
+        for b in range(REQUESTS + LAG):
+            if b < REQUESTS and b % GROUP == 0:
+                prefix_scores(b // GROUP)
+                arena = arena_pool.tile([BLOCK, 4, TOKENS], F32, tag="arena", name="arena")
+            if b < REQUESTS:
+                softmax_rows(b, arena)
+            if b >= LAG:
+                weighted_values(b - LAG, arena)

@@ -14,10 +14,21 @@ FEATURES = 128
 SLOTS = 4096
 BLOCK = 128
 QBLOCKS = TOKENS // BLOCK
-GROUP = 4
+UNITS = REQUESTS * QBLOCKS
+LOADED = 4
+RUN = 4
+SCORE_BANKS = 3
+OUT_BANK = 3
+BANK_BYTES = 2048
 SCALE = 0.08838834764831845
 MASKED = -1.0e30
-LAG = 2
+
+LOWS_LAG = 1
+NORMALISE_LAG = 3
+FLIP_LAG = 6
+KEEP_LAG = 7
+VALUES_LAG = 9
+STORE_LAG = 10
 
 FLOPS = REQUESTS * 2 * 2 * FEATURES * (TOKENS * (TOKENS + 1) // 2 + TOKENS * PREFIX)
 
@@ -26,22 +37,23 @@ def tile_radixattention_b_kernel(tc, table, q, k, v, vp, offs, out):
     nc = tc.nc
     with (
         tc.tile_pool(name="held", bufs=1) as held,
-        tc.tile_pool(name="rows", bufs=2 * GROUP) as rows,
-        tc.tile_pool(name="work", bufs=3) as work,
-        tc.psum_pool(name="arena", bufs=1) as arena_pool,
-        tc.psum_pool(name="flipped", bufs=4) as flipped_pool,
+        tc.tile_pool(name="stats", bufs=8 * QBLOCKS) as stats,
+        tc.tile_pool(name="rows", bufs=8) as rows,
+        tc.tile_pool(name="work", bufs=4) as work,
+        tc.psum_pool(name="shared_banks", bufs=1) as shared_banks,
+        tc.psum_pool(name="flip_bank", bufs=4) as flip_bank,
     ):
         offsets = held.tile([128, REQUESTS * PREFIX // 16], U16, name="offsets")
         nc.sync.dma_start(offsets[:], offs)
         pool_sb = held.tile([FEATURES, SLOTS], BF16, name="pool_sb")
 
         q_sb, k_sb, v_sb, vp_sb = [], [], [], []
-        for g in range(REQUESTS // GROUP):
-            first, last = g * GROUP, (g + 1) * GROUP
-            q_sb.append(held.tile([FEATURES, GROUP, TOKENS], BF16, name=f"q{g}"))
-            k_sb.append(held.tile([FEATURES, GROUP, TOKENS], BF16, name=f"k{g}"))
-            v_sb.append(held.tile([BLOCK, GROUP * QBLOCKS, FEATURES], BF16, name=f"v{g}"))
-            vp_sb.append(held.tile([PREFIX, GROUP, FEATURES], BF16, name=f"vp{g}"))
+        for g in range(REQUESTS // LOADED):
+            first, last = g * LOADED, (g + 1) * LOADED
+            q_sb.append(held.tile([FEATURES, LOADED, TOKENS], BF16, name=f"q{g}"))
+            k_sb.append(held.tile([FEATURES, LOADED, TOKENS], BF16, name=f"k{g}"))
+            v_sb.append(held.tile([BLOCK, LOADED * QBLOCKS, FEATURES], BF16, name=f"v{g}"))
+            vp_sb.append(held.tile([PREFIX, LOADED, FEATURES], BF16, name=f"vp{g}"))
             nc.sync.dma_start(q_sb[g][:], q[first:last].rearrange("b d e -> d b e"))
             if g == 0:
                 nc.sync.dma_start(pool_sb[:], table)
@@ -58,95 +70,110 @@ def tile_radixattention_b_kernel(tc, table, q, k, v, vp, offs, out):
             base=0, pattern=[[-1, BLOCK]], channel_multiplier=1,
         )
 
-        negated, prefix_low, weights = {}, {}, {}
+        score_ps, negated, prefix_low, low, exps, total, weights = {}, {}, {}, {}, {}, {}, {}
+        flipped_ps, flipped, out_ps = {}, {}, {}
 
         def query_block(b, i):
-            return q_sb[b // GROUP][:, b % GROUP, i * BLOCK : (i + 1) * BLOCK]
+            return q_sb[b // LOADED][:, b % LOADED, i * BLOCK : (i + 1) * BLOCK]
 
-        def prefix_scores(g):
-            prefix_ps = arena_pool.tile([BLOCK, GROUP, TOKENS], F32, tag="arena", name="prefix_ps")
-            for r in range(GROUP):
-                b = g * GROUP + r
+        def gather_run(first):
+            for b in range(first, first + RUN):
+                bank = (OUT_BANK + b - first) % (SCORE_BANKS + 1)
+                prefix_ps = shared_banks.tile(
+                    [BLOCK, QBLOCKS, PREFIX], F32, name=f"prefix_ps{bank}", offset=bank * BANK_BYTES
+                )
                 page_table = offsets[:, b * PREFIX // 16 : (b + 1) * PREFIX // 16]
                 for i in range(QBLOCKS):
                     nc.tensor.matmul(
-                        prefix_ps[:, r, i * BLOCK : (i + 1) * BLOCK],
-                        query_block(b, i),
-                        pool_sb[:].indirect(page_table),
+                        prefix_ps[:, i, :], query_block(b, i), pool_sb[:].indirect(page_table),
                         start=True, stop=True,
                     )
-            for r in range(GROUP):
-                b = g * GROUP + r
-                negated[b] = [
-                    rows.tile([BLOCK, PREFIX + (i + 1) * BLOCK], F32, name=f"negated{i}")
-                    for i in range(QBLOCKS)
-                ]
-                prefix_low[b] = rows.tile([BLOCK, QBLOCKS], F32, name="prefix_low")
                 for i in range(QBLOCKS):
+                    u = b * QBLOCKS + i
+                    negated[u] = rows.tile([BLOCK, PREFIX + (i + 1) * BLOCK], F32, name=f"negated{i}")
+                    prefix_low[u] = stats.tile([BLOCK, 1], F32, name="prefix_low")
                     nc.vector.tensor_scalar(
-                        out=negated[b][i][:, 0:PREFIX],
-                        in0=prefix_ps[:, r, i * BLOCK : (i + 1) * BLOCK],
-                        scalar1=-SCALE, scalar2=None, op0=ALU.mult, op1=ALU.min,
-                        accum_out=prefix_low[b][:, i : i + 1],
+                        out=negated[u][:, 0:PREFIX], in0=prefix_ps[:, i, :],
+                        scalar1=-SCALE, scalar2=None, op0=ALU.mult, op1=ALU.min, accum_out=prefix_low[u][:],
                     )
 
-        def softmax_rows(b, arena):
-            keys = k_sb[b // GROUP][:, b % GROUP, :]
-            low = rows.tile([BLOCK, QBLOCKS], F32, name="low")
-            total = rows.tile([BLOCK, QBLOCKS], F32, name="total")
-            exps = []
-            for i in range(QBLOCKS):
-                width = (i + 1) * BLOCK
-                bank = (b * QBLOCKS + i) % 3
-                nc.tensor.matmul(arena[:, bank, 0:width], query_block(b, i), keys[:, 0:width], start=True, stop=False)
-                nc.tensor.matmul(arena[:, bank, i * BLOCK : width], identity[:], causal[:], start=False, stop=True)
-                nc.vector.tensor_scalar(
-                    out=negated[b][i][:, PREFIX : PREFIX + width],
-                    in0=arena[:, bank, 0:width],
-                    scalar1=-SCALE, scalar2=prefix_low[b][:, i : i + 1], op0=ALU.mult, op1=ALU.min,
-                    accum_out=low[:, i : i + 1],
-                )
-                exps.append(work.tile([BLOCK, PREFIX + width], F32, name=f"exps{i}"))
-                nc.scalar.activation(
-                    out=exps[i][:], in_=negated[b][i][:], func=EXP,
-                    bias=low[:, i : i + 1], scale=-1.0, accum_out=total[:, i : i + 1],
-                )
-            factor = rows.tile([BLOCK, QBLOCKS], F32, name="factor")
-            nc.vector.reciprocal(factor[:], total[:])
-            weights[b] = []
-            for i in range(QBLOCKS):
-                weights[b].append(work.tile([BLOCK, PREFIX + (i + 1) * BLOCK], BF16, name=f"weights{i}"))
-                nc.gpsimd.tensor_scalar(
-                    out=weights[b][i][:], in0=exps[i][:],
-                    scalar1=factor[:, i : i + 1], scalar2=1.0, op0=ALU.mult, op1=ALU.mult,
-                )
+        def causal_scores(u):
+            b, i = divmod(u, QBLOCKS)
+            width = (i + 1) * BLOCK
+            bank = u % (RUN * QBLOCKS) % SCORE_BANKS
+            score_ps[u] = shared_banks.tile([BLOCK, width], F32, name=f"score_ps{bank}", offset=bank * BANK_BYTES)
+            nc.tensor.matmul(
+                score_ps[u][:], query_block(b, i), k_sb[b // LOADED][:, b % LOADED, 0:width],
+                start=True, stop=False,
+            )
+            nc.tensor.matmul(score_ps[u][:, i * BLOCK : width], identity[:], causal[:], start=False, stop=True)
 
-        def weighted_values(b, arena):
-            flipped = work.tile([BLOCK, 1 + QBLOCKS, TOKENS], BF16, name="flipped")
-            for i in range(QBLOCKS):
-                flipped_ps = flipped_pool.tile([BLOCK, 1 + QBLOCKS, BLOCK], BF16, name="flipped_ps")
-                for j in range(i + 2):
-                    nc.tensor.transpose(flipped_ps[:, j, :], weights[b][i][:, j * BLOCK : (j + 1) * BLOCK], identity[:])
-                nc.scalar.copy(out=flipped[:, 0 : i + 2, i * BLOCK : (i + 1) * BLOCK], in_=flipped_ps[:, 0 : i + 2, :])
-            out_ps = arena[:, 3, :]
-            nc.tensor.matmul(out_ps, vp_sb[b // GROUP][:, b % GROUP, :], flipped[:, 0, :], start=True, stop=False)
+        def row_lows(u):
+            low[u] = stats.tile([BLOCK, 1], F32, name="low")
+            nc.vector.tensor_scalar(
+                out=negated[u][:, PREFIX:], in0=score_ps[u][:],
+                scalar1=-SCALE, scalar2=prefix_low[u][:], op0=ALU.mult, op1=ALU.min, accum_out=low[u][:],
+            )
+
+        def exponentials(u):
+            exps[u] = work.tile(negated[u].shape, F32, name=f"exps{u % QBLOCKS}")
+            total[u] = stats.tile([BLOCK, 1], F32, name="total")
+            nc.scalar.activation(
+                out=exps[u][:], in_=negated[u][:], func=EXP, bias=low[u][:], scale=-1.0, accum_out=total[u][:],
+            )
+
+        def normalise(u):
+            factor = stats.tile([BLOCK, 1], F32, name="factor")
+            nc.vector.reciprocal(factor[:], total[u][:])
+            weights[u] = work.tile(exps[u].shape, BF16, name=f"weights{u % QBLOCKS}")
+            nc.gpsimd.tensor_scalar(
+                out=weights[u][:], in0=exps[u][:], scalar1=factor[:], scalar2=1.0, op0=ALU.mult, op1=ALU.mult,
+            )
+
+        def flip(u):
+            i = u % QBLOCKS
+            flipped_ps[u] = flip_bank.tile([BLOCK, 1 + QBLOCKS, BLOCK], BF16, name="flipped_ps")
+            for j in range(i + 2):
+                nc.tensor.transpose(flipped_ps[u][:, j, :], weights[u][:, j * BLOCK : (j + 1) * BLOCK], identity[:])
+
+        def keep_flipped(u):
+            b, i = divmod(u, QBLOCKS)
+            if i == 0:
+                flipped[b] = work.tile([BLOCK, 1 + QBLOCKS, TOKENS], BF16, name="flipped")
+            nc.vector.tensor_copy(flipped[b][:, 0 : i + 2, i * BLOCK : (i + 1) * BLOCK], flipped_ps[u][:, 0 : i + 2, :])
+
+        def weighted_values(b):
+            out_ps[b] = shared_banks.tile([FEATURES, TOKENS], F32, name="out_ps", offset=OUT_BANK * BANK_BYTES)
+            nc.tensor.matmul(out_ps[b][:], vp_sb[b // LOADED][:, b % LOADED, :], flipped[b][:, 0, :], start=True, stop=False)
             for j in range(QBLOCKS):
                 nc.tensor.matmul(
-                    arena[:, 3, j * BLOCK : TOKENS],
-                    v_sb[b // GROUP][:, (b % GROUP) * QBLOCKS + j, :],
-                    flipped[:, 1 + j, j * BLOCK : TOKENS],
+                    out_ps[b][:, j * BLOCK : TOKENS],
+                    v_sb[b // LOADED][:, (b % LOADED) * QBLOCKS + j, :],
+                    flipped[b][:, 1 + j, j * BLOCK : TOKENS],
                     start=False, stop=(j == QBLOCKS - 1),
                 )
+
+        def store(b):
             out_sb = work.tile([FEATURES, TOKENS], F32, name="out_sb")
-            nc.vector.tensor_copy(out_sb[:], out_ps)
+            nc.scalar.copy(out=out_sb[:], in_=out_ps[b][:])
             nc.sync.dma_start(out[b], out_sb[:])
 
-        arena = None
-        for b in range(REQUESTS + LAG):
-            if b < REQUESTS and b % GROUP == 0:
-                prefix_scores(b // GROUP)
-                arena = arena_pool.tile([BLOCK, 4, TOKENS], F32, tag="arena", name="arena")
-            if b < REQUESTS:
-                softmax_rows(b, arena)
-            if b >= LAG:
-                weighted_values(b - LAG, arena)
+        def unit_step(step, u):
+            if 0 <= u < UNITS:
+                step(u)
+
+        def request_step(step, u):
+            if 0 <= u < UNITS and u % QBLOCKS == QBLOCKS - 1:
+                step(u // QBLOCKS)
+
+        for t in range(UNITS + STORE_LAG):
+            unit_step(row_lows, t - LOWS_LAG)
+            unit_step(exponentials, t - LOWS_LAG)
+            if t < UNITS and t % (RUN * QBLOCKS) == 0:
+                gather_run(t // QBLOCKS)
+            unit_step(causal_scores, t)
+            unit_step(normalise, t - NORMALISE_LAG)
+            unit_step(flip, t - FLIP_LAG)
+            unit_step(keep_flipped, t - KEEP_LAG)
+            request_step(weighted_values, t - VALUES_LAG)
+            request_step(store, t - STORE_LAG)

@@ -17,8 +17,7 @@ QBLOCKS = TOKENS // BLOCK
 UNITS = REQUESTS * QBLOCKS
 LOADED = 4
 RUN = 4
-SCORE_BANKS = 3
-OUT_BANK = 3
+SHARED_BANKS = 4
 BANK_BYTES = 2048
 SCALE = 0.08838834764831845
 MASKED = -1.0e30
@@ -27,8 +26,8 @@ LOWS_LAG = 1
 NORMALISE_LAG = 3
 FLIP_LAG = 6
 KEEP_LAG = 7
-VALUES_LAG = 9
-STORE_LAG = 10
+VALUES_LAG = 13
+STORE_LAG = 14
 
 FLOPS = REQUESTS * 2 * 2 * FEATURES * (TOKENS * (TOKENS + 1) // 2 + TOKENS * PREFIX)
 
@@ -73,15 +72,19 @@ def tile_radixattention_b_kernel(tc, table, q, k, v, vp, offs, out):
         score_ps, negated, prefix_low, low, exps, total, weights = {}, {}, {}, {}, {}, {}, {}
         flipped_ps, flipped, out_ps = {}, {}, {}
 
+        handed_out = [0]
+
+        def next_bank(shape, name):
+            bank = handed_out[0] % SHARED_BANKS
+            handed_out[0] += 1
+            return shared_banks.tile(shape, F32, name=f"{name}{bank}", offset=bank * BANK_BYTES)
+
         def query_block(b, i):
             return q_sb[b // LOADED][:, b % LOADED, i * BLOCK : (i + 1) * BLOCK]
 
         def gather_run(first):
             for b in range(first, first + RUN):
-                bank = (OUT_BANK + b - first) % (SCORE_BANKS + 1)
-                prefix_ps = shared_banks.tile(
-                    [BLOCK, QBLOCKS, PREFIX], F32, name=f"prefix_ps{bank}", offset=bank * BANK_BYTES
-                )
+                prefix_ps = next_bank([BLOCK, QBLOCKS, PREFIX], "prefix_ps")
                 page_table = offsets[:, b * PREFIX // 16 : (b + 1) * PREFIX // 16]
                 for i in range(QBLOCKS):
                     nc.tensor.matmul(
@@ -100,8 +103,7 @@ def tile_radixattention_b_kernel(tc, table, q, k, v, vp, offs, out):
         def causal_scores(u):
             b, i = divmod(u, QBLOCKS)
             width = (i + 1) * BLOCK
-            bank = u % (RUN * QBLOCKS) % SCORE_BANKS
-            score_ps[u] = shared_banks.tile([BLOCK, width], F32, name=f"score_ps{bank}", offset=bank * BANK_BYTES)
+            score_ps[u] = next_bank([BLOCK, width], "score_ps")
             nc.tensor.matmul(
                 score_ps[u][:], query_block(b, i), k_sb[b // LOADED][:, b % LOADED, 0:width],
                 start=True, stop=False,
@@ -126,9 +128,14 @@ def tile_radixattention_b_kernel(tc, table, q, k, v, vp, offs, out):
             factor = stats.tile([BLOCK, 1], F32, name="factor")
             nc.vector.reciprocal(factor[:], total[u][:])
             weights[u] = work.tile(exps[u].shape, BF16, name=f"weights{u % QBLOCKS}")
-            nc.gpsimd.tensor_scalar(
-                out=weights[u][:], in0=exps[u][:], scalar1=factor[:], scalar2=1.0, op0=ALU.mult, op1=ALU.mult,
-            )
+            if u % QBLOCKS == 0:
+                nc.vector.tensor_scalar(
+                    out=weights[u][:], in0=exps[u][:], scalar1=factor[:], scalar2=None, op0=ALU.mult,
+                )
+            else:
+                nc.gpsimd.tensor_scalar(
+                    out=weights[u][:], in0=exps[u][:], scalar1=factor[:], scalar2=1.0, op0=ALU.mult, op1=ALU.mult,
+                )
 
         def flip(u):
             i = u % QBLOCKS
@@ -143,7 +150,7 @@ def tile_radixattention_b_kernel(tc, table, q, k, v, vp, offs, out):
             nc.vector.tensor_copy(flipped[b][:, 0 : i + 2, i * BLOCK : (i + 1) * BLOCK], flipped_ps[u][:, 0 : i + 2, :])
 
         def weighted_values(b):
-            out_ps[b] = shared_banks.tile([FEATURES, TOKENS], F32, name="out_ps", offset=OUT_BANK * BANK_BYTES)
+            out_ps[b] = next_bank([FEATURES, TOKENS], "out_ps")
             nc.tensor.matmul(out_ps[b][:], vp_sb[b // LOADED][:, b % LOADED, :], flipped[b][:, 0, :], start=True, stop=False)
             for j in range(QBLOCKS):
                 nc.tensor.matmul(
@@ -171,9 +178,9 @@ def tile_radixattention_b_kernel(tc, table, q, k, v, vp, offs, out):
             unit_step(exponentials, t - LOWS_LAG)
             if t < UNITS and t % (RUN * QBLOCKS) == 0:
                 gather_run(t // QBLOCKS)
+            request_step(weighted_values, t - VALUES_LAG)
             unit_step(causal_scores, t)
             unit_step(normalise, t - NORMALISE_LAG)
             unit_step(flip, t - FLIP_LAG)
             unit_step(keep_flipped, t - KEEP_LAG)
-            request_step(weighted_values, t - VALUES_LAG)
             request_step(store, t - STORE_LAG)

@@ -22,10 +22,12 @@ BANK_BYTES = 2048
 SCALE = 0.08838834764831845
 MASKED = -1.0e30
 
-LOWS_LAG = 1
-NORMALISE_LAG = 3
-FLIP_LAG = 6
-KEEP_LAG = 7
+TAKE_LAG = 1
+RUN_LAG = 4
+EXP_LAG = 4
+NORMALISE_LAG = 6
+FLIP_LAG = 9
+KEEP_LAG = 10
 VALUES_LAG = 13
 STORE_LAG = 14
 
@@ -48,17 +50,28 @@ def tile_radixattention_b_kernel(tc, table, q, k, v, vp, offs, out):
 
         q_sb, k_sb, v_sb, vp_sb = [], [], [], []
         for g in range(REQUESTS // LOADED):
-            first, last = g * LOADED, (g + 1) * LOADED
             q_sb.append(held.tile([FEATURES, LOADED, TOKENS], BF16, name=f"q{g}"))
             k_sb.append(held.tile([FEATURES, LOADED, TOKENS], BF16, name=f"k{g}"))
             v_sb.append(held.tile([BLOCK, LOADED * QBLOCKS, FEATURES], BF16, name=f"v{g}"))
             vp_sb.append(held.tile([PREFIX, LOADED, FEATURES], BF16, name=f"vp{g}"))
-            nc.sync.dma_start(q_sb[g][:], q[first:last].rearrange("b d e -> d b e"))
-            if g == 0:
-                nc.sync.dma_start(pool_sb[:], table)
-            nc.sync.dma_start(k_sb[g][:], k[first:last].rearrange("b d t -> d b t"))
+
+        def load_queries_and_keys(first, last):
+            g, a, b = first // LOADED, first % LOADED, first % LOADED + last - first
+            nc.sync.dma_start(q_sb[g][:, a:b, :], q[first:last].rearrange("b d e -> d b e"))
+            nc.sync.dma_start(k_sb[g][:, a:b, :], k[first:last].rearrange("b d t -> d b t"))
+
+        def load_values(g):
+            first, last = g * LOADED, (g + 1) * LOADED
             nc.sync.dma_start(v_sb[g][:], v[first:last].rearrange("b (j p) d -> p (b j) d", p=BLOCK))
             nc.sync.dma_start(vp_sb[g][:], vp[first:last].rearrange("b r d -> r b d"))
+
+        load_queries_and_keys(0, 1)
+        nc.sync.dma_start(pool_sb[:], table)
+        load_queries_and_keys(1, LOADED)
+        load_values(0)
+        for g in range(1, REQUESTS // LOADED):
+            load_queries_and_keys(g * LOADED, (g + 1) * LOADED)
+            load_values(g)
 
         identity = held.tile([BLOCK, BLOCK], BF16, name="identity")
         make_identity(nc, identity[:])
@@ -69,7 +82,7 @@ def tile_radixattention_b_kernel(tc, table, q, k, v, vp, offs, out):
             base=0, pattern=[[-1, BLOCK]], channel_multiplier=1,
         )
 
-        score_ps, negated, prefix_low, low, exps, total, weights = {}, {}, {}, {}, {}, {}, {}
+        score_ps, negated, low, exps, total, weights = {}, {}, {}, {}, {}, {}
         flipped_ps, flipped, out_ps = {}, {}, {}
 
         handed_out = [0]
@@ -82,6 +95,17 @@ def tile_radixattention_b_kernel(tc, table, q, k, v, vp, offs, out):
         def query_block(b, i):
             return q_sb[b // LOADED][:, b % LOADED, i * BLOCK : (i + 1) * BLOCK]
 
+        def take_scores(u, first_column, scores):
+            if u not in negated:
+                width = PREFIX + (u % QBLOCKS + 1) * BLOCK
+                negated[u] = rows.tile([BLOCK, width], F32, name=f"negated{u % QBLOCKS}")
+            low_before = low[u][:] if u in low else None
+            low[u] = stats.tile([BLOCK, 1], F32, name="low")
+            nc.vector.tensor_scalar(
+                out=negated[u][:, first_column : first_column + scores.shape[-1]], in0=scores,
+                scalar1=-SCALE, scalar2=low_before, op0=ALU.mult, op1=ALU.min, accum_out=low[u][:],
+            )
+
         def gather_run(first):
             for b in range(first, first + RUN):
                 prefix_ps = next_bank([BLOCK, QBLOCKS, PREFIX], "prefix_ps")
@@ -92,13 +116,7 @@ def tile_radixattention_b_kernel(tc, table, q, k, v, vp, offs, out):
                         start=True, stop=True,
                     )
                 for i in range(QBLOCKS):
-                    u = b * QBLOCKS + i
-                    negated[u] = rows.tile([BLOCK, PREFIX + (i + 1) * BLOCK], F32, name=f"negated{i}")
-                    prefix_low[u] = stats.tile([BLOCK, 1], F32, name="prefix_low")
-                    nc.vector.tensor_scalar(
-                        out=negated[u][:, 0:PREFIX], in0=prefix_ps[:, i, :],
-                        scalar1=-SCALE, scalar2=None, op0=ALU.mult, op1=ALU.min, accum_out=prefix_low[u][:],
-                    )
+                    take_scores(b * QBLOCKS + i, 0, prefix_ps[:, i, :])
 
         def causal_scores(u):
             b, i = divmod(u, QBLOCKS)
@@ -110,12 +128,8 @@ def tile_radixattention_b_kernel(tc, table, q, k, v, vp, offs, out):
             )
             nc.tensor.matmul(score_ps[u][:, i * BLOCK : width], identity[:], causal[:], start=False, stop=True)
 
-        def row_lows(u):
-            low[u] = stats.tile([BLOCK, 1], F32, name="low")
-            nc.vector.tensor_scalar(
-                out=negated[u][:, PREFIX:], in0=score_ps[u][:],
-                scalar1=-SCALE, scalar2=prefix_low[u][:], op0=ALU.mult, op1=ALU.min, accum_out=low[u][:],
-            )
+        def take_causal_scores(u):
+            take_scores(u, PREFIX, score_ps[u][:])
 
         def exponentials(u):
             exps[u] = work.tile(negated[u].shape, F32, name=f"exps{u % QBLOCKS}")
@@ -174,10 +188,10 @@ def tile_radixattention_b_kernel(tc, table, q, k, v, vp, offs, out):
                 step(u // QBLOCKS)
 
         for t in range(UNITS + STORE_LAG):
-            unit_step(row_lows, t - LOWS_LAG)
-            unit_step(exponentials, t - LOWS_LAG)
-            if t < UNITS and t % (RUN * QBLOCKS) == 0:
-                gather_run(t // QBLOCKS)
+            unit_step(take_causal_scores, t - TAKE_LAG)
+            if 0 <= t - RUN_LAG < UNITS and (t - RUN_LAG) % (RUN * QBLOCKS) == 0:
+                gather_run((t - RUN_LAG) // QBLOCKS)
+            unit_step(exponentials, t - EXP_LAG)
             request_step(weighted_values, t - VALUES_LAG)
             unit_step(causal_scores, t)
             unit_step(normalise, t - NORMALISE_LAG)

@@ -22,12 +22,12 @@ BANK_BYTES = 2048
 SCALE = 0.08838834764831845
 MASKED = -1.0e30
 
+EARLY = QBLOCKS
+
 TAKE_LAG = 1
-RUN_LAG = 4
-EXP_LAG = 4
-NORMALISE_LAG = 6
-FLIP_LAG = 9
-KEEP_LAG = 10
+NORMALISE_LAG = 3
+FLIP_LAG = 6
+KEEP_LAG = 7
 VALUES_LAG = 13
 STORE_LAG = 14
 
@@ -187,13 +187,19 @@ def tile_radixattention_b_kernel(tc, table, q, k, v, vp, offs, out):
             if 0 <= u < UNITS and u % QBLOCKS == QBLOCKS - 1:
                 step(u // QBLOCKS)
 
+        for u in range(EARLY):
+            causal_scores(u)
+            take_causal_scores(u)
+
         for t in range(UNITS + STORE_LAG):
-            unit_step(take_causal_scores, t - TAKE_LAG)
-            if 0 <= t - RUN_LAG < UNITS and (t - RUN_LAG) % (RUN * QBLOCKS) == 0:
-                gather_run((t - RUN_LAG) // QBLOCKS)
-            unit_step(exponentials, t - EXP_LAG)
+            if t - TAKE_LAG >= EARLY:
+                unit_step(take_causal_scores, t - TAKE_LAG)
+            unit_step(exponentials, t - TAKE_LAG)
+            if t < UNITS and t % (RUN * QBLOCKS) == 0:
+                gather_run(t // QBLOCKS)
             request_step(weighted_values, t - VALUES_LAG)
-            unit_step(causal_scores, t)
+            if t >= EARLY:
+                unit_step(causal_scores, t)
             unit_step(normalise, t - NORMALISE_LAG)
             unit_step(flip, t - FLIP_LAG)
             unit_step(keep_flipped, t - KEEP_LAG)

@@ -17,7 +17,8 @@ QBLOCKS = TOKENS // BLOCK
 UNITS = REQUESTS * QBLOCKS
 LOADED = 4
 RUN = 4
-SHARED_BANKS = 4
+SHARED_BANKS = 5
+FLIP_BANKS = 3
 BANK_BYTES = 2048
 SCALE = 0.08838834764831845
 MASKED = -1.0e30
@@ -42,7 +43,7 @@ def tile_radixattention_b_kernel(tc, table, q, k, v, vp, offs, out):
         tc.tile_pool(name="rows", bufs=8) as rows,
         tc.tile_pool(name="work", bufs=4) as work,
         tc.psum_pool(name="shared_banks", bufs=1) as shared_banks,
-        tc.psum_pool(name="flip_bank", bufs=4) as flip_bank,
+        tc.psum_pool(name="flip_bank", bufs=FLIP_BANKS) as flip_bank,
     ):
         offsets = held.tile([128, REQUESTS * PREFIX // 16], U16, name="offsets")
         nc.sync.dma_start(offsets[:], offs)
@@ -85,12 +86,12 @@ def tile_radixattention_b_kernel(tc, table, q, k, v, vp, offs, out):
         score_ps, negated, low, exps, total, weights = {}, {}, {}, {}, {}, {}
         flipped_ps, flipped, out_ps = {}, {}, {}
 
-        handed_out = [0]
+        in_turn = [SHARED_BANKS - 1]
+        latest = [-1]
 
         def next_bank(shape, name):
-            bank = handed_out[0] % SHARED_BANKS
-            handed_out[0] += 1
-            return shared_banks.tile(shape, F32, name=f"{name}{bank}", offset=bank * BANK_BYTES)
+            latest[0] = (latest[0] + 1) % in_turn[0]
+            return shared_banks.tile(shape, F32, name=f"{name}{latest[0]}", offset=latest[0] * BANK_BYTES)
 
         def query_block(b, i):
             return q_sb[b // LOADED][:, b % LOADED, i * BLOCK : (i + 1) * BLOCK]
@@ -164,6 +165,7 @@ def tile_radixattention_b_kernel(tc, table, q, k, v, vp, offs, out):
             nc.vector.tensor_copy(flipped[b][:, 0 : i + 2, i * BLOCK : (i + 1) * BLOCK], flipped_ps[u][:, 0 : i + 2, :])
 
         def weighted_values(b):
+            in_turn[0] = SHARED_BANKS
             out_ps[b] = next_bank([FEATURES, TOKENS], "out_ps")
             nc.tensor.matmul(out_ps[b][:], vp_sb[b // LOADED][:, b % LOADED, :], flipped[b][:, 0, :], start=True, stop=False)
             for j in range(QBLOCKS):

@@ -143,14 +143,9 @@ def tile_radixattention_b_kernel(tc, table, q, k, v, vp, offs, out):
             factor = stats.tile([BLOCK, 1], F32, name="factor")
             nc.vector.reciprocal(factor[:], total[u][:])
             weights[u] = work.tile(exps[u].shape, BF16, name=f"weights{u % QBLOCKS}")
-            if u % QBLOCKS == 0:
-                nc.vector.tensor_scalar(
-                    out=weights[u][:], in0=exps[u][:], scalar1=factor[:], scalar2=None, op0=ALU.mult,
-                )
-            else:
-                nc.gpsimd.tensor_scalar(
-                    out=weights[u][:], in0=exps[u][:], scalar1=factor[:], scalar2=1.0, op0=ALU.mult, op1=ALU.mult,
-                )
+            nc.gpsimd.tensor_scalar(
+                out=weights[u][:], in0=exps[u][:], scalar1=factor[:], scalar2=1.0, op0=ALU.mult, op1=ALU.mult,
+            )
 
         def flip(u):
             i = u % QBLOCKS

@@ -143,9 +143,12 @@ def tile_radixattention_b_kernel(tc, table, q, k, v, vp, offs, out):
             factor = stats.tile([BLOCK, 1], F32, name="factor")
             nc.vector.reciprocal(factor[:], total[u][:])
             weights[u] = work.tile(exps[u].shape, BF16, name=f"weights{u % QBLOCKS}")
-            nc.gpsimd.tensor_scalar(
-                out=weights[u][:], in0=exps[u][:], scalar1=factor[:], scalar2=1.0, op0=ALU.mult, op1=ALU.mult,
-            )
+            if u % (2 * QBLOCKS) == QBLOCKS:
+                nc.scalar.mul(out=weights[u][:], in_=exps[u][:], mul=factor[:])
+            else:
+                nc.gpsimd.tensor_scalar(
+                    out=weights[u][:], in0=exps[u][:], scalar1=factor[:], scalar2=1.0, op0=ALU.mult, op1=ALU.mult,
+                )
 
         def flip(u):
             i = u % QBLOCKS
@@ -159,22 +162,34 @@ def tile_radixattention_b_kernel(tc, table, q, k, v, vp, offs, out):
                 flipped[b] = work.tile([BLOCK, 1 + QBLOCKS, TOKENS], BF16, name="flipped")
             nc.vector.tensor_copy(flipped[b][:, 0 : i + 2, i * BLOCK : (i + 1) * BLOCK], flipped_ps[u][:, 0 : i + 2, :])
 
+        def output_parts(b):
+            if b < REQUESTS - 1:
+                return [(0, QBLOCKS)]
+            return [(0, QBLOCKS - 1), (QBLOCKS - 1, QBLOCKS)]
+
+        def values_of(b, g):
+            if g == 0:
+                return vp_sb[b // LOADED][:, b % LOADED, :]
+            return v_sb[b // LOADED][:, (b % LOADED) * QBLOCKS + g - 1, :]
+
         def weighted_values(b):
             in_turn[0] = SHARED_BANKS
-            out_ps[b] = next_bank([FEATURES, TOKENS], "out_ps")
-            nc.tensor.matmul(out_ps[b][:], vp_sb[b // LOADED][:, b % LOADED, :], flipped[b][:, 0, :], start=True, stop=False)
-            for j in range(QBLOCKS):
-                nc.tensor.matmul(
-                    out_ps[b][:, j * BLOCK : TOKENS],
-                    v_sb[b // LOADED][:, (b % LOADED) * QBLOCKS + j, :],
-                    flipped[b][:, 1 + j, j * BLOCK : TOKENS],
-                    start=False, stop=(j == QBLOCKS - 1),
-                )
+            for first, last in output_parts(b):
+                out_ps[b, first] = next_bank([FEATURES, (last - first) * BLOCK], "out_ps")
+                for g in range(last + 1):
+                    seen_from = max(first, g - 1)
+                    nc.tensor.matmul(
+                        out_ps[b, first][:, (seen_from - first) * BLOCK :],
+                        values_of(b, g),
+                        flipped[b][:, g, seen_from * BLOCK : last * BLOCK],
+                        start=(g == 0), stop=(g == last),
+                    )
 
         def store(b):
-            out_sb = work.tile([FEATURES, TOKENS], F32, name="out_sb")
-            nc.scalar.copy(out=out_sb[:], in_=out_ps[b][:])
-            nc.sync.dma_start(out[b], out_sb[:])
+            for first, last in output_parts(b):
+                out_sb = work.tile([FEATURES, (last - first) * BLOCK], F32, name="out_sb")
+                nc.scalar.copy(out=out_sb[:], in_=out_ps[b, first][:])
+                nc.sync.dma_start(out[b][:, first * BLOCK : last * BLOCK], out_sb[:])
 
         def unit_step(step, u):
             if 0 <= u < UNITS:

@@ -17,8 +17,9 @@ QBLOCKS = TOKENS // BLOCK
 UNITS = REQUESTS * QBLOCKS
 LOADED = 4
 RUN = 4
-SHARED_BANKS = 5
-FLIP_BANKS = 3
+SHARED_BANKS = 6
+BANKS_AT_START = 4
+FLIP_BANKS = 2
 BANK_BYTES = 2048
 SCALE = 0.08838834764831845
 MASKED = -1.0e30
@@ -86,12 +87,15 @@ def tile_radixattention_b_kernel(tc, table, q, k, v, vp, offs, out):
         score_ps, negated, low, exps, total, weights = {}, {}, {}, {}, {}, {}
         flipped_ps, flipped, out_ps = {}, {}, {}
 
-        in_turn = [SHARED_BANKS - 1]
-        latest = [-1]
+        in_turn = list(range(BANKS_AT_START))
+        unused = list(range(BANKS_AT_START, SHARED_BANKS))
 
-        def next_bank(shape, name):
-            latest[0] = (latest[0] + 1) % in_turn[0]
-            return shared_banks.tile(shape, F32, name=f"{name}{latest[0]}", offset=latest[0] * BANK_BYTES)
+        def next_bank(shape, name, may_open=False):
+            source = unused if may_open and unused else in_turn
+            bank = source[0]
+            source.remove(bank)
+            in_turn.append(bank)
+            return shared_banks.tile(shape, F32, name=f"{name}{bank}", offset=bank * BANK_BYTES)
 
         def query_block(b, i):
             return q_sb[b // LOADED][:, b % LOADED, i * BLOCK : (i + 1) * BLOCK]
@@ -173,9 +177,8 @@ def tile_radixattention_b_kernel(tc, table, q, k, v, vp, offs, out):
             return v_sb[b // LOADED][:, (b % LOADED) * QBLOCKS + g - 1, :]
 
         def weighted_values(b):
-            in_turn[0] = SHARED_BANKS
             for first, last in output_parts(b):
-                out_ps[b, first] = next_bank([FEATURES, (last - first) * BLOCK], "out_ps")
+                out_ps[b, first] = next_bank([FEATURES, (last - first) * BLOCK], "out_ps", may_open=True)
                 for g in range(last + 1):
                     seen_from = max(first, g - 1)
                     nc.tensor.matmul(

import concourse.mybir as mybir
from concourse.masks import make_identity

F32 = mybir.dt.float32
BF16 = mybir.dt.bfloat16
U16 = mybir.dt.uint16
ALU = mybir.AluOpType
EXP = mybir.ActivationFunctionType.Exp

REQUESTS = 16
TOKENS = 512
PREFIX = 128
FEATURES = 128
SLOTS = 4096
BLOCK = 128
QBLOCKS = TOKENS // BLOCK
UNITS = REQUESTS * QBLOCKS
LOADED = 4
RUN = 4
SHARED_BANKS = 6
BANKS_AT_START = 4
FLIP_BANKS = 2
BANK_BYTES = 2048
SCALE = 0.08838834764831845
MASKED = -1.0e30

EARLY = QBLOCKS

TAKE_LAG = 1
NORMALISE_LAG = 3
FLIP_LAG = 6
KEEP_LAG = 7
VALUES_LAG = 13
STORE_LAG = 14

FLOPS = REQUESTS * 2 * 2 * FEATURES * (TOKENS * (TOKENS + 1) // 2 + TOKENS * PREFIX)


def tile_radixattention_b_kernel(tc, table, q, k, v, vp, offs, out):
    nc = tc.nc
    with (
        tc.tile_pool(name="held", bufs=1) as held,
        tc.tile_pool(name="stats", bufs=8 * QBLOCKS) as stats,
        tc.tile_pool(name="rows", bufs=8) as rows,
        tc.tile_pool(name="work", bufs=4) as work,
        tc.psum_pool(name="shared_banks", bufs=1) as shared_banks,
        tc.psum_pool(name="flip_bank", bufs=FLIP_BANKS) as flip_bank,
    ):
        offsets = held.tile([128, REQUESTS * PREFIX // 16], U16, name="offsets")
        nc.sync.dma_start(offsets[:], offs)
        pool_sb = held.tile([FEATURES, SLOTS], BF16, name="pool_sb")

        q_sb, k_sb, v_sb, vp_sb = [], [], [], []
        for g in range(REQUESTS // LOADED):
            q_sb.append(held.tile([FEATURES, LOADED, TOKENS], BF16, name=f"q{g}"))
            k_sb.append(held.tile([FEATURES, LOADED, TOKENS], BF16, name=f"k{g}"))
            v_sb.append(held.tile([BLOCK, LOADED * QBLOCKS, FEATURES], BF16, name=f"v{g}"))
            vp_sb.append(held.tile([PREFIX, LOADED, FEATURES], BF16, name=f"vp{g}"))

        def load_queries_and_keys(first, last):
            g, a, b = first // LOADED, first % LOADED, first % LOADED + last - first
            nc.sync.dma_start(q_sb[g][:, a:b, :], q[first:last].rearrange("b d e -> d b e"))
            nc.sync.dma_start(k_sb[g][:, a:b, :], k[first:last].rearrange("b d t -> d b t"))

        def load_values(g):
            first, last = g * LOADED, (g + 1) * LOADED
            nc.sync.dma_start(v_sb[g][:], v[first:last].rearrange("b (j p) d -> p (b j) d", p=BLOCK))
            nc.sync.dma_start(vp_sb[g][:], vp[first:last].rearrange("b r d -> r b d"))

        load_queries_and_keys(0, 1)
        nc.sync.dma_start(pool_sb[:], table)
        load_queries_and_keys(1, LOADED)
        load_values(0)
        for g in range(1, REQUESTS // LOADED):
            load_queries_and_keys(g * LOADED, (g + 1) * LOADED)
            load_values(g)

        identity = held.tile([BLOCK, BLOCK], BF16, name="identity")
        make_identity(nc, identity[:])
        causal = held.tile([BLOCK, BLOCK], BF16, name="causal")
        nc.gpsimd.memset(causal[:], 0.0)
        nc.gpsimd.affine_select(
            out=causal[:], in_=causal[:], compare_op=ALU.is_ge, fill=MASKED,
            base=0, pattern=[[-1, BLOCK]], channel_multiplier=1,
        )

        score_ps, negated, low, exps, total, weights = {}, {}, {}, {}, {}, {}
        flipped_ps, flipped, out_ps = {}, {}, {}

        in_turn = list(range(BANKS_AT_START))
        unused = list(range(BANKS_AT_START, SHARED_BANKS))

        def next_bank(shape, name, may_open=False):
            source = unused if may_open and unused else in_turn
            bank = source[0]
            source.remove(bank)
            in_turn.append(bank)
            return shared_banks.tile(shape, F32, name=f"{name}{bank}", offset=bank * BANK_BYTES)

        def query_block(b, i):
            return q_sb[b // LOADED][:, b % LOADED, i * BLOCK : (i + 1) * BLOCK]

        def take_scores(u, first_column, scores):
            if u not in negated:
                width = PREFIX + (u % QBLOCKS + 1) * BLOCK
                negated[u] = rows.tile([BLOCK, width], F32, name=f"negated{u % QBLOCKS}")
            low_before = low[u][:] if u in low else None
            low[u] = stats.tile([BLOCK, 1], F32, name="low")
            nc.vector.tensor_scalar(
                out=negated[u][:, first_column : first_column + scores.shape[-1]], in0=scores,
                scalar1=-SCALE, scalar2=low_before, op0=ALU.mult, op1=ALU.min, accum_out=low[u][:],
            )

        def gather_run(first):
            for b in range(first, first + RUN):
                prefix_ps = next_bank([BLOCK, QBLOCKS, PREFIX], "prefix_ps")
                page_table = offsets[:, b * PREFIX // 16 : (b + 1) * PREFIX // 16]
                for i in range(QBLOCKS):
                    nc.tensor.matmul(
                        prefix_ps[:, i, :], query_block(b, i), pool_sb[:].indirect(page_table),
                        start=True, stop=True,
                    )
                for i in range(QBLOCKS):
                    take_scores(b * QBLOCKS + i, 0, prefix_ps[:, i, :])

        def causal_scores(u):
            b, i = divmod(u, QBLOCKS)
            width = (i + 1) * BLOCK
            score_ps[u] = next_bank([BLOCK, width], "score_ps")
            nc.tensor.matmul(
                score_ps[u][:], query_block(b, i), k_sb[b // LOADED][:, b % LOADED, 0:width],
                start=True, stop=False,
            )
            nc.tensor.matmul(score_ps[u][:, i * BLOCK : width], identity[:], causal[:], start=False, stop=True)

        def take_causal_scores(u):
            take_scores(u, PREFIX, score_ps[u][:])

        def exponentials(u):
            exps[u] = work.tile(negated[u].shape, F32, name=f"exps{u % QBLOCKS}")
            total[u] = stats.tile([BLOCK, 1], F32, name="total")
            nc.scalar.activation(
                out=exps[u][:], in_=negated[u][:], func=EXP, bias=low[u][:], scale=-1.0, accum_out=total[u][:],
            )

        def normalise(u):
            factor = stats.tile([BLOCK, 1], F32, name="factor")
            nc.vector.reciprocal(factor[:], total[u][:])
            weights[u] = work.tile(exps[u].shape, BF16, name=f"weights{u % QBLOCKS}")
            if u % (2 * QBLOCKS) == QBLOCKS:
                nc.scalar.mul(out=weights[u][:], in_=exps[u][:], mul=factor[:])
            else:
                nc.gpsimd.tensor_scalar(
                    out=weights[u][:], in0=exps[u][:], scalar1=factor[:], scalar2=1.0, op0=ALU.mult, op1=ALU.mult,
                )

        def flip(u):
            i = u % QBLOCKS
            flipped_ps[u] = flip_bank.tile([BLOCK, 1 + QBLOCKS, BLOCK], BF16, name="flipped_ps")
            for j in range(i + 2):
                nc.tensor.transpose(flipped_ps[u][:, j, :], weights[u][:, j * BLOCK : (j + 1) * BLOCK], identity[:])

        def keep_flipped(u):
            b, i = divmod(u, QBLOCKS)
            if i == 0:
                flipped[b] = work.tile([BLOCK, 1 + QBLOCKS, TOKENS], BF16, name="flipped")
            nc.vector.tensor_copy(flipped[b][:, 0 : i + 2, i * BLOCK : (i + 1) * BLOCK], flipped_ps[u][:, 0 : i + 2, :])

        def output_parts(b):
            if b < REQUESTS - 1:
                return [(0, QBLOCKS)]
            return [(0, QBLOCKS - 1), (QBLOCKS - 1, QBLOCKS)]

        def values_of(b, g):
            if g == 0:
                return vp_sb[b // LOADED][:, b % LOADED, :]
            return v_sb[b // LOADED][:, (b % LOADED) * QBLOCKS + g - 1, :]

        def weighted_values(b):
            for first, last in output_parts(b):
                out_ps[b, first] = next_bank([FEATURES, (last - first) * BLOCK], "out_ps", may_open=True)
                for g in range(last + 1):
                    seen_from = max(first, g - 1)
                    nc.tensor.matmul(
                        out_ps[b, first][:, (seen_from - first) * BLOCK :],
                        values_of(b, g),
                        flipped[b][:, g, seen_from * BLOCK : last * BLOCK],
                        start=(g == 0), stop=(g == last),
                    )

        def store(b):
            for first, last in output_parts(b):
                out_sb = work.tile([FEATURES, (last - first) * BLOCK], F32, name="out_sb")
                nc.scalar.copy(out=out_sb[:], in_=out_ps[b, first][:])
                nc.sync.dma_start(out[b][:, first * BLOCK : last * BLOCK], out_sb[:])

        def unit_step(step, u):
            if 0 <= u < UNITS:
                step(u)

        def request_step(step, u):
            if 0 <= u < UNITS and u % QBLOCKS == QBLOCKS - 1:
                step(u // QBLOCKS)

        for u in range(EARLY):
            causal_scores(u)
            take_causal_scores(u)

        for t in range(UNITS + STORE_LAG):
            if t - TAKE_LAG >= EARLY:
                unit_step(take_causal_scores, t - TAKE_LAG)
            unit_step(exponentials, t - TAKE_LAG)
            if t < UNITS and t % (RUN * QBLOCKS) == 0:
                gather_run(t // QBLOCKS)
            request_step(weighted_values, t - VALUES_LAG)
            if t >= EARLY:
                unit_step(causal_scores, t)
            unit_step(normalise, t - NORMALISE_LAG)
            unit_step(flip, t - FLIP_LAG)
            unit_step(keep_flipped, t - KEEP_LAG)
            request_step(store, t - STORE_LAG)
